import numpy as np
import ml_dtypes


def mxq(x, axis, fmt="e4m3"):
    dtype, down = {"e4m3": (ml_dtypes.float8_e4m3fn, 7), "e5m2": (ml_dtypes.float8_e5m2, 14)}[fmt]
    v = np.moveaxis(np.asarray(x, np.float32).astype(ml_dtypes.bfloat16).astype(np.float64), axis, -1)
    blocks = v.reshape(v.shape[:-1] + (-1, 32))
    amax = np.abs(blocks).max(-1, keepdims=True)
    byte = np.maximum(np.where(amax > 0, np.frexp(amax)[1] - 1 + 127, 0) - down, 1)
    scale = np.exp2(byte - 127.0)
    codes = (blocks / scale).astype(np.float32).astype(dtype).astype(np.float64)
    return np.moveaxis((codes * scale).reshape(v.shape), -1, axis)


WIDE = False


def mx_kscale(k):
    if not WIDE:
        return np.ones(k)
    levels = np.array([10, -10, 5, -5, 0])
    a = np.random.permutation(np.resize(levels, k // 512 * 4)).reshape(k // 512, 4)
    idx = np.arange(k)
    return np.exp2(a[idx // 512, idx % 128 // 32])


BF16 = ml_dtypes.bfloat16


def bf(x):
    return np.asarray(x, np.float32).astype(BF16)


def f64(x):
    return np.asarray(x).astype(np.float64)


E2M1 = np.array([0.0, 0.5, 1.0, 1.5, 2.0, 3.0, 4.0, 6.0, -0.0, -0.5, -1.0, -1.5, -2.0, -3.0, -4.0, -6.0])


def pack_weight(w, fmt):
    k, n = w.shape
    w = f64(bf(w)).reshape(k // 32, 32, n)
    amax = np.abs(w).max(1)
    if fmt == "e4m3":
        byte = np.frexp(amax)[1] - 1 + 127 - 7
    else:
        mant, ex = np.frexp(amax / 6.0)
        byte = np.where(mant > 0.5, ex, ex - 1) + 127
    byte = np.clip(np.where(amax > 0, byte, 1), 1, 254)
    scaled = (w * np.exp2(127.0 - byte)[:, None, :]).reshape(k, n).astype(np.float32)
    by_word = np.ascontiguousarray(scaled.reshape(k // 512, 128, 4, n).transpose(0, 1, 3, 2))
    if fmt == "e4m3":
        words = by_word.astype(ml_dtypes.float8_e4m3fn).view(np.uint8)
    else:
        c = by_word.astype(ml_dtypes.float4_e2m1fn).view(np.uint8) & 0xF
        words = c[..., 0::2] | (c[..., 1::2] << 4)
    return np.ascontiguousarray(words), np.ascontiguousarray(byte.astype(np.uint8).reshape(k // 512, 16, n))


def unpack_weight(words, scales, fmt):
    g, p, n, _ = words.shape
    if fmt == "e4m3":
        vals = np.ascontiguousarray(words).view(ml_dtypes.float8_e4m3fn).astype(np.float64)
    else:
        nib = np.empty((g, p, n, 4), np.uint8)
        nib[..., 0::2] = words & 0xF
        nib[..., 1::2] = words >> 4
        vals = E2M1[nib]
    vals = vals * np.repeat(np.exp2(scales.astype(np.float64) - 127.0), 8, axis=1)[..., None]
    return vals.transpose(0, 1, 3, 2).reshape(g * 512, n)


B, L, D, H = 4, 512, 1024, 16
DH = D // H


def setup_inputs():
    s, t = mx_kscale(D), mx_kscale(L)
    row = 1.0 / np.sqrt(np.arange(L) + 1.0)
    x = bf(np.random.standard_normal((B, L, D)) * s * t[:, None])
    words, scales = pack_weight((np.random.standard_normal((D, D)) / np.sqrt(D) / s).T, "e4m3")
    mat2a = bf(np.random.standard_normal((H, L, L)) * row[:, None] / t)
    return {"x": x,
            "W1a_words": words,
            "W1a_scales": scales,
            "mat2a": mat2a}


def reference(x, W1a_words, W1a_scales, mat2a):
    p = mxq(f64(x), 2, "e4m3") @ unpack_weight(W1a_words, W1a_scales, "e4m3")
    ph = p.reshape(B, L, H, DH).transpose(0, 2, 1, 3)
    tril_a = np.tril(f64(mat2a)[:, :L, :L])
    y = mxq(tril_a, 2, "e4m3") @ mxq(ph, 2, "e4m3")
    y = np.maximum(y, 0.0)
    return y.transpose(0, 2, 1, 3).reshape(B, L, D)

@@ -1,0 +1,259 @@
+from contextlib import ExitStack
+
+import concourse.mybir as mybir
+from concourse.masks import make_identity
+
+F32 = mybir.dt.float32
+BF16 = mybir.dt.bfloat16
+I32 = mybir.dt.int32
+U32 = mybir.dt.uint32
+U8 = mybir.dt.uint8
+FP8X4 = mybir.dt.float8_e4m3fn_x4
+ALU = mybir.AluOpType
+ACT = mybir.ActivationFunctionType
+
+B, L, D, H = 4, 512, 1024, 16
+DH = D // H
+P = 128
+PACK = 4
+K_PASS = P * PACK
+G = D // K_PASS
+PAIR = 2
+WORDS = K_PASS // PAIR
+LB = L // P
+CHUNK = 128
+CHUNK_HEADS = CHUNK // DH
+N_CHUNKS = D // CHUNK
+QUARTER = 2 * CHUNK
+QUARTER_HEADS = QUARTER // DH
+MIX_N = B * DH
+HEAD_CHUNKS = 3
+ROUND_BANKS = 3
+
+FLOPS = 2 * B * L * D * D + B * H * DH * L * (L + 1)
+BYTES = 2 * B * L * D + D * D + D * D // 32 + H * L * (L + 1) + 4 * B * L * D
+
+
+def tile_causal_kron_block_mlp_pa_kernel(tc, x, W1a_words, W1a_scales, mat2a, out):
+    nc = tc.nc
+    with ExitStack() as ctx:
+        ctx.enter_context(tc.manual_schedule())
+        keep = ctx.enter_context(tc.tile_pool(name="keep", bufs=1))
+        grouped_pool = ctx.enter_context(tc.tile_pool(name="grouped", bufs=3))
+        p_pool = ctx.enter_context(tc.tile_pool(name="p_grouped", bufs=HEAD_CHUNKS + 1))
+        codes_pool = ctx.enter_context(tc.tile_pool(name="codes", bufs=6))
+        y_pool = ctx.enter_context(tc.tile_pool(name="y", bufs=2 * LB))
+        low_pool = ctx.enter_context(tc.psum_pool(name="low", bufs=1))
+        banks = ctx.enter_context(tc.psum_pool(name="banks", bufs=6))
+
+        x_sb = [keep.tile([P, PACK, D], BF16, name="x_sb%d" % b) for b in range(B)]
+        x_codes = [keep.tile([P, PACK * G * P], U32, name="x_codes%d" % b, align_bytes=64) for b in range(B)]
+        x_scales = [keep.tile([P, PACK * G * P], U8, name="x_scales%d" % b, align_bytes=64) for b in range(B)]
+        w_codes = keep.tile([P, G, D], U32, name="w_codes", align_bytes=64)
+        w_scales = keep.tile([P, D], U8, name="w_scales", align_bytes=64)
+        nc.vector.memset(w_scales[:].bitcast(I32), 0)
+        a_sb = [keep.tile([P, H, 2 * P * (i // 2 + 1)], BF16, name="a_sb%d" % i) for i in range(LB)]
+        for i in range(0, LB, 2):
+            nc.vector.memset(a_sb[i][:, :, P * (i + 1):].bitcast(F32), 0.0)
+
+        ident = keep.tile([P, P], F32, name="ident")
+        make_identity(nc, ident[:])
+        zero_words = keep.tile([P, P], F32, name="zero_words")
+        nc.vector.memset(zero_words[:], 0.0)
+        tril_f32 = keep.tile([P, P], F32, name="tril_f32")
+        nc.gpsimd.memset(tril_f32[:], 1.0)
+        nc.gpsimd.affine_select(
+            out=tril_f32[:], in_=tril_f32[:], compare_op=ALU.is_ge, fill=0.0,
+            base=0, pattern=[[-1, P]], channel_multiplier=1,
+        )
+        tril = keep.tile([P, P], BF16, name="tril")
+        nc.vector.tensor_copy(out=tril[:], in_=tril_f32[:])
+
+        def load_x(b):
+            for u in range(2):
+                nc.sync.dma_start(
+                    out=x_sb[b][:, PAIR * u:PAIR * (u + 1), :],
+                    in_=x[b, 2 * P * u:2 * P * (u + 1), :].rearrange("(q e) k -> q e k", e=PAIR),
+                )
+
+        def load_w_half(half):
+            cols = slice(D // 2 * half, D // 2 * (half + 1))
+            nc.sync.dma_start(
+                out=w_codes[:, :, cols].bitcast(I32),
+                in_=W1a_words[:, :, cols, :].rearrange("g p n t -> p g (n t)").bitcast(I32),
+            )
+
+        def load_a(quarter):
+            heads = slice(QUARTER_HEADS * quarter, QUARTER_HEADS * (quarter + 1))
+            for i in range(LB):
+                nc.sync.dma_start(
+                    out=a_sb[i][:, heads, 0:P * (i + 1)],
+                    in_=mat2a[heads, P * i:P * (i + 1), 0:P * (i + 1)].rearrange("h l m -> l h m"),
+                )
+
+        load_x(0)
+        for quad in range(4):
+            nc.sync.dma_start(
+                out=w_scales[32 * quad:32 * quad + 4 * G, :].bitcast(I32),
+                in_=W1a_scales[:, 4 * quad:4 * quad + 4, :].bitcast(I32),
+            )
+        load_x(1)
+        load_w_half(0)
+        load_x(2)
+        load_x(3)
+        load_a(0)
+        load_w_half(1)
+        for quarter in range(1, D // QUARTER):
+            load_a(quarter)
+
+        low_banks = [low_pool.tile([P, 2, 2, P], F32, name="low_bank%d" % j) for j in range(2)]
+        for bank in low_banks:
+            for i in range(2):
+                nc.tensor.transpose(bank[:, 1, i, :], zero_words[:], ident[:])
+
+        def transpose_x_half(b, u):
+            grouped = grouped_pool.tile([P, PAIR * G * P * PACK], BF16, tag="x_grouped", align_bytes=64)
+            grouped_words = grouped[:].bitcast(F32).rearrange("p (e g q v) -> p e g q v", e=PAIR, g=G, v=2)
+            for e in range(PAIR):
+                x_words = x_sb[b][:, PAIR * u + e, :].bitcast(F32)
+                bank = banks.tile([P, G, 2, P], F32, tag="bank")
+                for g in range(G):
+                    for v in range(2):
+                        nc.tensor.transpose(
+                            bank[:, g, v, :], x_words[:, WORDS * g + v:WORDS * (g + 1):2], ident[:]
+                        )
+                copy = nc.scalar.copy if e == 0 else nc.vector.tensor_copy
+                copy(out=grouped_words[:, e], in_=bank[:].rearrange("p g v q -> p g q v"))
+            return grouped
+
+        def quantise_x_half(b, u, grouped):
+            cols = slice(PAIR * G * P * u, PAIR * G * P * (u + 1))
+            nc.vector.quantize_mx(
+                out=x_codes[b][:, cols].bitcast(FP8X4), scales=x_scales[b][:, cols], in_=grouped[:]
+            )
+
+        p_grouped = {}
+        p_mx = {}
+
+        def project_bank(c, b):
+            cols = slice(CHUNK * c, CHUNK * (c + 1))
+            if c not in p_grouped:
+                p_grouped[c] = p_pool.tile(
+                    [P, CHUNK_HEADS, B, DH, PACK], BF16, name="p_grouped", tag="p_grouped", align_bytes=64
+                )
+            bank = banks.tile([P, PACK, CHUNK], F32, tag="bank")
+            for t in range(PACK):
+                for g in range(G):
+                    tokens = slice((t * G + g) * P, (t * G + g + 1) * P)
+                    nc.tensor.matmul_mx(
+                        out=bank[:, t, :],
+                        lhsT=x_codes[b][:, tokens].bitcast(FP8X4),
+                        lhsT_scale=x_scales[b][:, tokens],
+                        rhs=w_codes[:, g, cols].bitcast(FP8X4),
+                        rhs_scale=w_scales[4 * g:P, cols],
+                        start=(g == 0),
+                        stop=(g == G - 1),
+                    )
+            nc.scalar.copy(
+                out=p_grouped[c][:, :, b, :, :],
+                in_=bank[:].rearrange("p t (h d) -> p h d t", h=CHUNK_HEADS),
+            )
+            if b == B - 1:
+                codes = codes_pool.tile([P, CHUNK_HEADS * MIX_N], U32, tag="p_codes", align_bytes=64)
+                scales = codes_pool.tile([P, CHUNK_HEADS * MIX_N], U8, tag="p_scales", align_bytes=64)
+                nc.vector.quantize_mx(
+                    out=codes[:].bitcast(FP8X4), scales=scales[:],
+                    in_=p_grouped[c][:].rearrange("p h b d t -> p (h b d t)"),
+                )
+                p_mx[c] = (codes, scales)
+
+        def mask_a(quarter):
+            heads = slice(QUARTER_HEADS * quarter, QUARTER_HEADS * (quarter + 1))
+            for i in range(LB):
+                diagonal = a_sb[i][:, heads, P * i:P * (i + 1)]
+                nc.vector.tensor_tensor(
+                    out=diagonal, in0=diagonal,
+                    in1=tril[:].unsqueeze(1).to_broadcast([P, QUARTER_HEADS, P]), op=ALU.mult,
+                )
+
+        def transpose_a(h):
+            grouped = grouped_pool.tile([P, LB * P * PACK], BF16, tag="a_grouped", align_bytes=64)
+            grouped_words = grouped[:].bitcast(F32).rearrange("p (i l u) -> p i l u", i=LB, u=2)
+            low = low_banks[h % 2]
+            for i in range(2):
+                nc.tensor.transpose(low[:, 0, i, :], a_sb[i][:, h, :].bitcast(F32), ident[:])
+            nc.scalar.copy(out=grouped_words[:, 0:2], in_=low[:].rearrange("p u i l -> p i l u"))
+            high = banks.tile([P, 2, 2, P], F32, tag="bank")
+            for i in range(2):
+                for u in range(2):
+                    nc.tensor.transpose(
+                        high[:, u, i, :], a_sb[2 + i][:, h, :].bitcast(F32)[:, P * u:P * (u + 1)], ident[:]
+                    )
+            nc.vector.tensor_copy(out=grouped_words[:, 2:4], in_=high[:].rearrange("p u i l -> p i l u"))
+            return grouped
+
+        def quantise_a(grouped):
+            codes = codes_pool.tile([P, L], U32, tag="a_codes", align_bytes=64)
+            scales = codes_pool.tile([P, L], U8, tag="a_scales", align_bytes=64)
+            nc.vector.quantize_mx(out=codes[:].bitcast(FP8X4), scales=scales[:], in_=grouped[:])
+            return codes, scales
+
+        def mix(c, a_mx, y):
+            p_codes, p_scales = p_mx[c]
+            y_cols = slice(CHUNK * (c % 2), CHUNK * (c % 2 + 1))
+            for i in range(LB):
+                rows = slice(P * i, P * (i + 1))
+                bank = banks.tile([P, CHUNK_HEADS, MIX_N], F32, tag="bank")
+                for j in range(CHUNK_HEADS):
+                    a_codes, a_scales = a_mx[j]
+                    head_cols = slice(MIX_N * j, MIX_N * (j + 1))
+                    nc.tensor.matmul_mx(
+                        out=bank[:, j, :],
+                        lhsT=a_codes[:, rows].bitcast(FP8X4),
+                        lhsT_scale=a_scales[:, rows],
+                        rhs=p_codes[:, head_cols].bitcast(FP8X4),
+                        rhs_scale=p_scales[:, head_cols],
+                        start=True,
+                        stop=True,
+                    )
+                y_view = y[i][:, :, y_cols].rearrange("p b (j d) -> p b j d", j=CHUNK_HEADS)
+                bank_view = bank[:].rearrange("p j (b d) -> p b j d", b=B)
+                if i < LB - 1:
+                    nc.scalar.activation(out=y_view, in_=bank_view, func=ACT.Relu)
+                else:
+                    nc.vector.tensor_scalar_max(out=y_view, in0=bank_view, scalar1=0.0)
+                if c % 2 == 1:
+                    cols = slice(QUARTER * (c // 2), QUARTER * (c // 2 + 1))
+                    nc.sync.dma_start(
+                        out=out[:, rows, cols].rearrange("b l n -> l b n"), in_=y[i][:]
+                    )
+
+        waiting = None
+        for b in range(B):
+            for u in range(2):
+                grouped = transpose_x_half(b, u)
+                if waiting is not None:
+                    quantise_x_half(*waiting)
+                waiting = (b, u, grouped)
+            if b > 0:
+                for c in range(HEAD_CHUNKS):
+                    project_bank(c, b - 1)
+        quantise_x_half(*waiting)
+        mask_a(0)
+
+        todo = [(c, B - 1) for c in range(HEAD_CHUNKS)]
+        todo += [(c, b) for c in range(HEAD_CHUNKS, N_CHUNKS) for b in range(B)]
+        a_mx = {}
+        y = None
+        for r in range(N_CHUNKS + 1):
+            if r < N_CHUNKS:
+                a_grouped = [transpose_a(CHUNK_HEADS * r + j) for j in range(CHUNK_HEADS)]
+                a_mx[r] = [quantise_a(grouped) for grouped in a_grouped]
+                if r % 2 == 1 and r + 1 < N_CHUNKS:
+                    mask_a((r + 1) // 2)
+            for c, b in todo[ROUND_BANKS * r:ROUND_BANKS * (r + 1)]:
+                project_bank(c, b)
+            if r > 0:
+                if (r - 1) % 2 == 0:
+                    y = [y_pool.tile([P, B, QUARTER], F32, tag="y", name="y%d" % i) for i in range(LB)]
+                mix(r - 1, a_mx[r - 1], y)

@@ -189,7 +189,8 @@ def tile_causal_kron_block_mlp_pa_kernel(tc, x, W1a_words, W1a_scales, mat2a, ou
                     nc.tensor.transpose(
                         high[:, u, i, :], a_sb[2 + i][:, h, :].bitcast(F32)[:, P * u:P * (u + 1)], ident[:]
                     )
-            nc.vector.tensor_copy(out=grouped_words[:, 2:4], in_=high[:].rearrange("p u i l -> p i l u"))
+            copy = nc.vector.tensor_copy if h % 2 == 0 else nc.scalar.copy
+            copy(out=grouped_words[:, 2:4], in_=high[:].rearrange("p u i l -> p i l u"))
             return grouped
 
         def quantise_a(grouped):
@@ -218,7 +219,7 @@ def tile_causal_kron_block_mlp_pa_kernel(tc, x, W1a_words, W1a_scales, mat2a, ou
                     )
                 y_view = y[i][:, :, y_cols].rearrange("p b (j d) -> p b j d", j=CHUNK_HEADS)
                 bank_view = bank[:].rearrange("p j (b d) -> p b j d", b=B)
-                if i < LB - 1:
+                if i % 2 == 0:
                     nc.scalar.activation(out=y_view, in_=bank_view, func=ACT.Relu)
                 else:
                     nc.vector.tensor_scalar_max(out=y_view, in0=bank_view, scalar1=0.0)
@@ -228,17 +229,12 @@ def tile_causal_kron_block_mlp_pa_kernel(tc, x, W1a_words, W1a_scales, mat2a, ou
                         out=out[:, rows, cols].rearrange("b l n -> l b n"), in_=y[i][:]
                     )
 
-        waiting = None
         for b in range(B):
             for u in range(2):
-                grouped = transpose_x_half(b, u)
-                if waiting is not None:
-                    quantise_x_half(*waiting)
-                waiting = (b, u, grouped)
+                quantise_x_half(b, u, transpose_x_half(b, u))
             if b > 0:
                 for c in range(HEAD_CHUNKS):
                     project_bank(c, b - 1)
-        quantise_x_half(*waiting)
         mask_a(0)
 
         todo = [(c, B - 1) for c in range(HEAD_CHUNKS)]
@@ -249,8 +245,8 @@ def tile_causal_kron_block_mlp_pa_kernel(tc, x, W1a_words, W1a_scales, mat2a, ou
             if r < N_CHUNKS:
                 a_grouped = [transpose_a(CHUNK_HEADS * r + j) for j in range(CHUNK_HEADS)]
                 a_mx[r] = [quantise_a(grouped) for grouped in a_grouped]
-                if r % 2 == 1 and r + 1 < N_CHUNKS:
-                    mask_a((r + 1) // 2)
+                if r % 2 == 0 and r + 2 < N_CHUNKS:
+                    mask_a(r // 2 + 1)
             for c, b in todo[ROUND_BANKS * r:ROUND_BANKS * (r + 1)]:
                 project_bank(c, b)
             if r > 0:

@@ -60,14 +60,6 @@ def tile_causal_kron_block_mlp_pa_kernel(tc, x, W1a_words, W1a_scales, mat2a, ou
         make_identity(nc, ident[:])
         zero_words = keep.tile([P, P], F32, name="zero_words")
         nc.vector.memset(zero_words[:], 0.0)
-        tril_f32 = keep.tile([P, P], F32, name="tril_f32")
-        nc.gpsimd.memset(tril_f32[:], 1.0)
-        nc.gpsimd.affine_select(
-            out=tril_f32[:], in_=tril_f32[:], compare_op=ALU.is_ge, fill=0.0,
-            base=0, pattern=[[-1, P]], channel_multiplier=1,
-        )
-        tril = keep.tile([P, P], BF16, name="tril")
-        nc.vector.tensor_copy(out=tril[:], in_=tril_f32[:])
 
         def load_x(b):
             for u in range(2):
@@ -171,9 +163,9 @@ def tile_causal_kron_block_mlp_pa_kernel(tc, x, W1a_words, W1a_scales, mat2a, ou
             heads = slice(QUARTER_HEADS * quarter, QUARTER_HEADS * (quarter + 1))
             for i in range(LB):
                 diagonal = a_sb[i][:, heads, P * i:P * (i + 1)]
-                nc.vector.tensor_tensor(
-                    out=diagonal, in0=diagonal,
-                    in1=tril[:].unsqueeze(1).to_broadcast([P, QUARTER_HEADS, P]), op=ALU.mult,
+                nc.gpsimd.affine_select(
+                    out=diagonal, in_=diagonal, compare_op=ALU.is_ge, fill=0.0,
+                    base=0, pattern=[[0, QUARTER_HEADS], [-1, P]], channel_multiplier=1,
                 )
 
         def transpose_a(h):
@@ -189,8 +181,7 @@ def tile_causal_kron_block_mlp_pa_kernel(tc, x, W1a_words, W1a_scales, mat2a, ou
                     nc.tensor.transpose(
                         high[:, u, i, :], a_sb[2 + i][:, h, :].bitcast(F32)[:, P * u:P * (u + 1)], ident[:]
                     )
-            copy = nc.vector.tensor_copy if h % 2 == 0 else nc.scalar.copy
-            copy(out=grouped_words[:, 2:4], in_=high[:].rearrange("p u i l -> p i l u"))
+            nc.vector.tensor_copy(out=grouped_words[:, 2:4], in_=high[:].rearrange("p u i l -> p i l u"))
             return grouped
 
         def quantise_a(grouped):
@@ -235,7 +226,8 @@ def tile_causal_kron_block_mlp_pa_kernel(tc, x, W1a_words, W1a_scales, mat2a, ou
             if b > 0:
                 for c in range(HEAD_CHUNKS):
                     project_bank(c, b - 1)
-        mask_a(0)
+        for quarter in range(D // QUARTER):
+            mask_a(quarter)
 
         todo = [(c, B - 1) for c in range(HEAD_CHUNKS)]
         todo += [(c, b) for c in range(HEAD_CHUNKS, N_CHUNKS) for b in range(B)]
@@ -245,8 +237,6 @@ def tile_causal_kron_block_mlp_pa_kernel(tc, x, W1a_words, W1a_scales, mat2a, ou
             if r < N_CHUNKS:
                 a_grouped = [transpose_a(CHUNK_HEADS * r + j) for j in range(CHUNK_HEADS)]
                 a_mx[r] = [quantise_a(grouped) for grouped in a_grouped]
-                if r % 2 == 0 and r + 2 < N_CHUNKS:
-                    mask_a(r // 2 + 1)
             for c, b in todo[ROUND_BANKS * r:ROUND_BANKS * (r + 1)]:
                 project_bank(c, b)
             if r > 0:

@@ -216,7 +216,8 @@ def tile_causal_kron_block_mlp_pa_kernel(tc, x, W1a_words, W1a_scales, mat2a, ou
                     nc.vector.tensor_scalar_max(out=y_view, in0=bank_view, scalar1=0.0)
                 if c % 2 == 1:
                     cols = slice(QUARTER * (c // 2), QUARTER * (c // 2 + 1))
-                    nc.sync.dma_start(
+                    queue = nc.scalar if i % 2 == 0 else nc.sync
+                    queue.dma_start(
                         out=out[:, rows, cols].rearrange("b l n -> l b n"), in_=y[i][:]
                     )
 

@@ -103,6 +103,13 @@ def tile_causal_kron_block_mlp_pa_kernel(tc, x, W1a_words, W1a_scales, mat2a, ou
             for i in range(2):
                 nc.tensor.transpose(bank[:, 1, i, :], zero_words[:], ident[:])
 
+        kept_back = []
+
+        def scalar_has_issued():
+            for y_tile, where in kept_back:
+                nc.scalar.dma_start(out=where, in_=y_tile[:])
+            kept_back.clear()
+
         def transpose_x_half(b, u):
             grouped = grouped_pool.tile([P, PAIR * G * P * PACK], BF16, tag="x_grouped", align_bytes=64)
             grouped_words = grouped[:].bitcast(F32).rearrange("p (e g q v) -> p e g q v", e=PAIR, g=G, v=2)
@@ -175,6 +182,7 @@ def tile_causal_kron_block_mlp_pa_kernel(tc, x, W1a_words, W1a_scales, mat2a, ou
             for i in range(2):
                 nc.tensor.transpose(low[:, 0, i, :], a_sb[i][:, h, :].bitcast(F32), ident[:])
             nc.scalar.copy(out=grouped_words[:, 0:2], in_=low[:].rearrange("p u i l -> p i l u"))
+            scalar_has_issued()
             high = banks.tile([P, 2, 2, P], F32, tag="bank")
             for i in range(2):
                 for u in range(2):
@@ -212,14 +220,16 @@ def tile_causal_kron_block_mlp_pa_kernel(tc, x, W1a_words, W1a_scales, mat2a, ou
                 bank_view = bank[:].rearrange("p j (b d) -> p b j d", b=B)
                 if i % 2 == 0:
                     nc.scalar.activation(out=y_view, in_=bank_view, func=ACT.Relu)
+                    scalar_has_issued()
                 else:
                     nc.vector.tensor_scalar_max(out=y_view, in0=bank_view, scalar1=0.0)
                 if c % 2 == 1:
                     cols = slice(QUARTER * (c // 2), QUARTER * (c // 2 + 1))
-                    queue = nc.scalar if i % 2 == 0 else nc.sync
-                    queue.dma_start(
-                        out=out[:, rows, cols].rearrange("b l n -> l b n"), in_=y[i][:]
-                    )
+                    where = out[:, rows, cols].rearrange("b l n -> l b n")
+                    if i % 2 == 0:
+                        kept_back.append((y[i], where))
+                    else:
+                        nc.sync.dma_start(out=where, in_=y[i][:])
 
         for b in range(B):
             for u in range(2):
@@ -244,3 +254,4 @@ def tile_causal_kron_block_mlp_pa_kernel(tc, x, W1a_words, W1a_scales, mat2a, ou
                 if (r - 1) % 2 == 0:
                     y = [y_pool.tile([P, B, QUARTER], F32, tag="y", name="y%d" % i) for i in range(LB)]
                 mix(r - 1, a_mx[r - 1], y)
+        scalar_has_issued()

from contextlib import ExitStack

import concourse.mybir as mybir
from concourse.masks import make_identity

F32 = mybir.dt.float32
BF16 = mybir.dt.bfloat16
I32 = mybir.dt.int32
U32 = mybir.dt.uint32
U8 = mybir.dt.uint8
FP8X4 = mybir.dt.float8_e4m3fn_x4
ALU = mybir.AluOpType
ACT = mybir.ActivationFunctionType

B, L, D, H = 4, 512, 1024, 16
DH = D // H
P = 128
PACK = 4
K_PASS = P * PACK
G = D // K_PASS
PAIR = 2
WORDS = K_PASS // PAIR
LB = L // P
CHUNK = 128
CHUNK_HEADS = CHUNK // DH
N_CHUNKS = D // CHUNK
QUARTER = 2 * CHUNK
QUARTER_HEADS = QUARTER // DH
MIX_N = B * DH
HEAD_CHUNKS = 3
ROUND_BANKS = 3

FLOPS = 2 * B * L * D * D + B * H * DH * L * (L + 1)
BYTES = 2 * B * L * D + D * D + D * D // 32 + H * L * (L + 1) + 4 * B * L * D


def tile_causal_kron_block_mlp_pa_kernel(tc, x, W1a_words, W1a_scales, mat2a, out):
    nc = tc.nc
    with ExitStack() as ctx:
        ctx.enter_context(tc.manual_schedule())
        keep = ctx.enter_context(tc.tile_pool(name="keep", bufs=1))
        grouped_pool = ctx.enter_context(tc.tile_pool(name="grouped", bufs=3))
        p_pool = ctx.enter_context(tc.tile_pool(name="p_grouped", bufs=HEAD_CHUNKS + 1))
        codes_pool = ctx.enter_context(tc.tile_pool(name="codes", bufs=6))
        y_pool = ctx.enter_context(tc.tile_pool(name="y", bufs=2 * LB))
        low_pool = ctx.enter_context(tc.psum_pool(name="low", bufs=1))
        banks = ctx.enter_context(tc.psum_pool(name="banks", bufs=6))

        x_sb = [keep.tile([P, PACK, D], BF16, name="x_sb%d" % b) for b in range(B)]
        x_codes = [keep.tile([P, PACK * G * P], U32, name="x_codes%d" % b, align_bytes=64) for b in range(B)]
        x_scales = [keep.tile([P, PACK * G * P], U8, name="x_scales%d" % b, align_bytes=64) for b in range(B)]
        w_codes = keep.tile([P, G, D], U32, name="w_codes", align_bytes=64)
        w_scales = keep.tile([P, D], U8, name="w_scales", align_bytes=64)
        nc.vector.memset(w_scales[:].bitcast(I32), 0)
        a_sb = [keep.tile([P, H, 2 * P * (i // 2 + 1)], BF16, name="a_sb%d" % i) for i in range(LB)]
        for i in range(0, LB, 2):
            nc.vector.memset(a_sb[i][:, :, P * (i + 1):].bitcast(F32), 0.0)

        ident = keep.tile([P, P], F32, name="ident")
        make_identity(nc, ident[:])
        zero_words = keep.tile([P, P], F32, name="zero_words")
        nc.vector.memset(zero_words[:], 0.0)

        def load_x(b):
            for u in range(2):
                nc.sync.dma_start(
                    out=x_sb[b][:, PAIR * u:PAIR * (u + 1), :],
                    in_=x[b, 2 * P * u:2 * P * (u + 1), :].rearrange("(q e) k -> q e k", e=PAIR),
                )

        def load_w_half(half):
            cols = slice(D // 2 * half, D // 2 * (half + 1))
            nc.sync.dma_start(
                out=w_codes[:, :, cols].bitcast(I32),
                in_=W1a_words[:, :, cols, :].rearrange("g p n t -> p g (n t)").bitcast(I32),
            )

        def load_a(quarter):
            heads = slice(QUARTER_HEADS * quarter, QUARTER_HEADS * (quarter + 1))
            for i in range(LB):
                nc.sync.dma_start(
                    out=a_sb[i][:, heads, 0:P * (i + 1)],
                    in_=mat2a[heads, P * i:P * (i + 1), 0:P * (i + 1)].rearrange("h l m -> l h m"),
                )

        load_x(0)
        for quad in range(4):
            nc.sync.dma_start(
                out=w_scales[32 * quad:32 * quad + 4 * G, :].bitcast(I32),
                in_=W1a_scales[:, 4 * quad:4 * quad + 4, :].bitcast(I32),
            )
        load_x(1)
        load_w_half(0)
        load_x(2)
        load_x(3)
        load_a(0)
        load_w_half(1)
        for quarter in range(1, D // QUARTER):
            load_a(quarter)

        low_banks = [low_pool.tile([P, 2, 2, P], F32, name="low_bank%d" % j) for j in range(2)]
        for bank in low_banks:
            for i in range(2):
                nc.tensor.transpose(bank[:, 1, i, :], zero_words[:], ident[:])

        kept_back = []

        def scalar_has_issued():
            for y_tile, where in kept_back:
                nc.scalar.dma_start(out=where, in_=y_tile[:])
            kept_back.clear()

        def transpose_x_half(b, u):
            grouped = grouped_pool.tile([P, PAIR * G * P * PACK], BF16, tag="x_grouped", align_bytes=64)
            grouped_words = grouped[:].bitcast(F32).rearrange("p (e g q v) -> p e g q v", e=PAIR, g=G, v=2)
            for e in range(PAIR):
                x_words = x_sb[b][:, PAIR * u + e, :].bitcast(F32)
                bank = banks.tile([P, G, 2, P], F32, tag="bank")
                for g in range(G):
                    for v in range(2):
                        nc.tensor.transpose(
                            bank[:, g, v, :], x_words[:, WORDS * g + v:WORDS * (g + 1):2], ident[:]
                        )
                copy = nc.scalar.copy if e == 0 else nc.vector.tensor_copy
                copy(out=grouped_words[:, e], in_=bank[:].rearrange("p g v q -> p g q v"))
            return grouped

        def quantise_x_half(b, u, grouped):
            cols = slice(PAIR * G * P * u, PAIR * G * P * (u + 1))
            nc.vector.quantize_mx(
                out=x_codes[b][:, cols].bitcast(FP8X4), scales=x_scales[b][:, cols], in_=grouped[:]
            )

        p_grouped = {}
        p_mx = {}

        def project_bank(c, b):
            cols = slice(CHUNK * c, CHUNK * (c + 1))
            if c not in p_grouped:
                p_grouped[c] = p_pool.tile(
                    [P, CHUNK_HEADS, B, DH, PACK], BF16, name="p_grouped", tag="p_grouped", align_bytes=64
                )
            bank = banks.tile([P, PACK, CHUNK], F32, tag="bank")
            for t in range(PACK):
                for g in range(G):
                    tokens = slice((t * G + g) * P, (t * G + g + 1) * P)
                    nc.tensor.matmul_mx(
                        out=bank[:, t, :],
                        lhsT=x_codes[b][:, tokens].bitcast(FP8X4),
                        lhsT_scale=x_scales[b][:, tokens],
                        rhs=w_codes[:, g, cols].bitcast(FP8X4),
                        rhs_scale=w_scales[4 * g:P, cols],
                        start=(g == 0),
                        stop=(g == G - 1),
                    )
            nc.scalar.copy(
                out=p_grouped[c][:, :, b, :, :],
                in_=bank[:].rearrange("p t (h d) -> p h d t", h=CHUNK_HEADS),
            )
            if b == B - 1:
                codes = codes_pool.tile([P, CHUNK_HEADS * MIX_N], U32, tag="p_codes", align_bytes=64)
                scales = codes_pool.tile([P, CHUNK_HEADS * MIX_N], U8, tag="p_scales", align_bytes=64)
                nc.vector.quantize_mx(
                    out=codes[:].bitcast(FP8X4), scales=scales[:],
                    in_=p_grouped[c][:].rearrange("p h b d t -> p (h b d t)"),
                )
                p_mx[c] = (codes, scales)

        def mask_a(quarter):
            heads = slice(QUARTER_HEADS * quarter, QUARTER_HEADS * (quarter + 1))
            for i in range(LB):
                diagonal = a_sb[i][:, heads, P * i:P * (i + 1)]
                nc.gpsimd.affine_select(
                    out=diagonal, in_=diagonal, compare_op=ALU.is_ge, fill=0.0,
                    base=0, pattern=[[0, QUARTER_HEADS], [-1, P]], channel_multiplier=1,
                )

        def transpose_a(h):
            grouped = grouped_pool.tile([P, LB * P * PACK], BF16, tag="a_grouped", align_bytes=64)
            grouped_words = grouped[:].bitcast(F32).rearrange("p (i l u) -> p i l u", i=LB, u=2)
            low = low_banks[h % 2]
            for i in range(2):
                nc.tensor.transpose(low[:, 0, i, :], a_sb[i][:, h, :].bitcast(F32), ident[:])
            nc.scalar.copy(out=grouped_words[:, 0:2], in_=low[:].rearrange("p u i l -> p i l u"))
            scalar_has_issued()
            high = banks.tile([P, 2, 2, P], F32, tag="bank")
            for i in range(2):
                for u in range(2):
                    nc.tensor.transpose(
                        high[:, u, i, :], a_sb[2 + i][:, h, :].bitcast(F32)[:, P * u:P * (u + 1)], ident[:]
                    )
            nc.vector.tensor_copy(out=grouped_words[:, 2:4], in_=high[:].rearrange("p u i l -> p i l u"))
            return grouped

        def quantise_a(grouped):
            codes = codes_pool.tile([P, L], U32, tag="a_codes", align_bytes=64)
            scales = codes_pool.tile([P, L], U8, tag="a_scales", align_bytes=64)
            nc.vector.quantize_mx(out=codes[:].bitcast(FP8X4), scales=scales[:], in_=grouped[:])
            return codes, scales

        def mix(c, a_mx, y):
            p_codes, p_scales = p_mx[c]
            y_cols = slice(CHUNK * (c % 2), CHUNK * (c % 2 + 1))
            for i in range(LB):
                rows = slice(P * i, P * (i + 1))
                bank = banks.tile([P, CHUNK_HEADS, MIX_N], F32, tag="bank")
                for j in range(CHUNK_HEADS):
                    a_codes, a_scales = a_mx[j]
                    head_cols = slice(MIX_N * j, MIX_N * (j + 1))
                    nc.tensor.matmul_mx(
                        out=bank[:, j, :],
                        lhsT=a_codes[:, rows].bitcast(FP8X4),
                        lhsT_scale=a_scales[:, rows],
                        rhs=p_codes[:, head_cols].bitcast(FP8X4),
                        rhs_scale=p_scales[:, head_cols],
                        start=True,
                        stop=True,
                    )
                y_view = y[i][:, :, y_cols].rearrange("p b (j d) -> p b j d", j=CHUNK_HEADS)
                bank_view = bank[:].rearrange("p j (b d) -> p b j d", b=B)
                if i % 2 == 0:
                    nc.scalar.activation(out=y_view, in_=bank_view, func=ACT.Relu)
                    scalar_has_issued()
                else:
                    nc.vector.tensor_scalar_max(out=y_view, in0=bank_view, scalar1=0.0)
                if c % 2 == 1:
                    cols = slice(QUARTER * (c // 2), QUARTER * (c // 2 + 1))
                    where = out[:, rows, cols].rearrange("b l n -> l b n")
                    if i % 2 == 0:
                        kept_back.append((y[i], where))
                    else:
                        nc.sync.dma_start(out=where, in_=y[i][:])

        for b in range(B):
            for u in range(2):
                quantise_x_half(b, u, transpose_x_half(b, u))
            if b > 0:
                for c in range(HEAD_CHUNKS):
                    project_bank(c, b - 1)
        for quarter in range(D // QUARTER):
            mask_a(quarter)

        todo = [(c, B - 1) for c in range(HEAD_CHUNKS)]
        todo += [(c, b) for c in range(HEAD_CHUNKS, N_CHUNKS) for b in range(B)]
        a_mx = {}
        y = None
        for r in range(N_CHUNKS + 1):
            if r < N_CHUNKS:
                a_grouped = [transpose_a(CHUNK_HEADS * r + j) for j in range(CHUNK_HEADS)]
                a_mx[r] = [quantise_a(grouped) for grouped in a_grouped]
            for c, b in todo[ROUND_BANKS * r:ROUND_BANKS * (r + 1)]:
                project_bank(c, b)
            if r > 0:
                if (r - 1) % 2 == 0:
                    y = [y_pool.tile([P, B, QUARTER], F32, tag="y", name="y%d" % i) for i in range(LB)]
                mix(r - 1, a_mx[r - 1], y)
        scalar_has_issued()
